import numpy as np
import ml_dtypes


def mxq(x, axis, fmt="e4m3"):
    dtype, down = {"e4m3": (ml_dtypes.float8_e4m3fn, 7), "e5m2": (ml_dtypes.float8_e5m2, 14)}[fmt]
    v = np.moveaxis(np.asarray(x, np.float32).astype(ml_dtypes.bfloat16).astype(np.float64), axis, -1)
    blocks = v.reshape(v.shape[:-1] + (-1, 32))
    amax = np.abs(blocks).max(-1, keepdims=True)
    byte = np.maximum(np.where(amax > 0, np.frexp(amax)[1] - 1 + 127, 0) - down, 1)
    scale = np.exp2(byte - 127.0)
    codes = (blocks / scale).astype(np.float32).astype(dtype).astype(np.float64)
    return np.moveaxis((codes * scale).reshape(v.shape), -1, axis)


WIDE = False


def mx_kscale(k):
    if not WIDE:
        return np.ones(k)
    levels = np.array([10, -10, 5, -5, 0])
    if k % 512:
        return np.exp2(np.random.permutation(np.resize(levels, k // 32))).repeat(32)
    a = np.empty((k // 512, 16))
    for p in range(k // 512):
        a[p, :8] = np.random.permutation(np.resize(levels, 8))
        for g in range(8):
            far = levels[np.abs(levels - a[p, g]) >= 10]
            a[p, g + 8] = far[np.random.randint(len(far))]
    return np.exp2(a.ravel()).repeat(32)


BF16 = ml_dtypes.bfloat16


def bf(x):
    return np.asarray(x, np.float32).astype(BF16)


def f64(x):
    return np.asarray(x).astype(np.float64)


B, N, I, E = 4, 128, 512, 512

EPS = 1e-07


def sigmoid(v):
    return 1.0 / (1.0 + np.exp(-v))


def setup_inputs():
    s = mx_kscale(E)
    c = np.sqrt(np.mean(s * s) * np.mean(1.0 / (s * s)))
    ru = np.exp(0.5 * np.random.standard_normal((B, N, 1)))
    ri = np.exp(0.5 * np.random.standard_normal((B, I, 1)))
    return {"user_emb": bf(np.random.standard_normal((B, N, E)) * ru * s),
            "item_emb": bf(np.random.standard_normal((B, I, E)) * ri / s),
            "proj_w": bf((1.5 + 0.1 * np.random.standard_normal((1, 1))) * np.sqrt(E) * c),
            "proj_b": bf(0.5 + 0.1 * np.random.standard_normal(1))}


def reference(user_emb, item_emb, proj_w, proj_b):
    user_emb, item_emb, proj_w, proj_b = f64(user_emb), f64(item_emb), f64(proj_w), f64(proj_b)
    u = user_emb / np.maximum(np.linalg.norm(user_emb, axis=-1, keepdims=True), EPS)
    v = item_emb / np.maximum(np.linalg.norm(item_emb, axis=-1, keepdims=True), EPS)
    cos_sim = mxq(v, 2, "e4m3") @ mxq(u, 2, "e4m3").transpose(0, 2, 1)
    return sigmoid(cos_sim * proj_w[0, 0] + proj_b[0])

@@ -1,0 +1,191 @@
+from contextlib import ExitStack
+
+import concourse.mybir as mybir
+from concourse.masks import make_identity
+
+F32 = mybir.dt.float32
+BF16 = mybir.dt.bfloat16
+U32 = mybir.dt.uint32
+U8 = mybir.dt.uint8
+FP8X4 = mybir.dt.float8_e4m3fn_x4
+ACT = mybir.ActivationFunctionType
+ALU = mybir.AluOpType
+
+P = 128
+BATCHES = 4
+USERS = 128
+ITEMS = 512
+EMB = 512
+EPS = 1e-07
+
+FLOPS = 2 * BATCHES * ITEMS * USERS * EMB
+
+ITEM_TILES = ITEMS // P
+ROW_TILES = BATCHES + BATCHES * ITEM_TILES
+PAIR = 2
+UNITS = ROW_TILES // PAIR
+USER_UNITS = BATCHES // PAIR
+HALVES = 2
+UNIT_COLS = PAIR * P
+
+INVERT_LAG = 1
+NORMALISE_LAG = 2
+QUANTISE_LAG = 3
+
+
+def tile_similarityoutputlayer_s_kernel(tc, user_emb, item_emb, proj_w, proj_b, out):
+    nc = tc.nc
+
+    def unit_rows(u):
+        if u < USER_UNITS:
+            return user_emb[PAIR * u : PAIR * u + PAIR].rearrange("b n k -> n b k")
+        b, half = divmod(u - USER_UNITS, ITEM_TILES // PAIR)
+        by_partition = item_emb[b].rearrange("(p c) k -> p c k", c=ITEM_TILES)
+        return by_partition[:, PAIR * half : PAIR * half + PAIR, :]
+
+    with ExitStack() as ctx:
+        const = ctx.enter_context(tc.tile_pool(name="const", bufs=1))
+        per_unit = ctx.enter_context(tc.tile_pool(name="per_unit", bufs=UNITS))
+        per_batch = ctx.enter_context(tc.tile_pool(name="per_batch", bufs=BATCHES))
+        flipped_banks = ctx.enter_context(tc.psum_pool(name="flipped_banks", bufs=4))
+        cos_banks = ctx.enter_context(tc.psum_pool(name="cos_banks", bufs=BATCHES))
+        ctx.enter_context(tc.manual_schedule())
+
+        minus_half = const.tile([P, PAIR], F32)
+        nc.gpsimd.memset(minus_half[:], -0.5)
+        identity = const.tile([P, P], F32)
+        make_identity(nc, identity[:])
+        gain_bf16 = const.tile([P, 1], BF16)
+        nc.gpsimd.dma_start(
+            out=gain_bf16[:], in_=proj_w.rearrange("a b -> (a b)").partition_broadcast(P)
+        )
+        bias_bf16 = const.tile([P, 1], BF16)
+        nc.gpsimd.dma_start(out=bias_bf16[:], in_=proj_b.partition_broadcast(P))
+        table_warmer = const.tile([P, 1], F32)
+        nc.scalar.activation(out=table_warmer[:], in_=minus_half[:, 0:1], func=ACT.Sigmoid)
+        gain = const.tile([P, 1], F32)
+        nc.vector.tensor_copy(out=gain[:], in_=gain_bf16[:])
+        bias = const.tile([P, 1], F32)
+        nc.vector.tensor_copy(out=bias[:], in_=bias_bf16[:])
+
+        codes = const.tile([P, ROW_TILES * P], U32, align_bytes=64)
+        scales = const.tile([P, ROW_TILES * P], U8, align_bytes=64)
+
+        raw, inverse_norm, flipped, grouped = {}, {}, {}, {}
+        sum_squares, cos = {}, {}
+
+        def load(u):
+            rows = per_unit.tile([P, PAIR, EMB], BF16)
+            nc.sync.dma_start(out=rows[:], in_=unit_rows(u))
+            raw[u] = rows
+
+        def squares(u):
+            unread = per_unit.tile([P, PAIR, EMB], BF16)
+            total = per_unit.tile([P, PAIR], F32)
+            for a in range(PAIR):
+                nc.scalar.activation(
+                    out=unread[:, a, :],
+                    in_=raw[u][:, a, :],
+                    func=ACT.Square,
+                    accum_out=total[:, a : a + 1],
+                )
+            sum_squares[u] = total
+
+        def invert(u):
+            clamped = per_unit.tile([P, PAIR], F32)
+            nc.gpsimd.tensor_scalar_max(out=clamped[:], in0=sum_squares[u][:], scalar1=EPS * EPS)
+            inverse = per_unit.tile([P, PAIR], F32)
+            nc.gpsimd.tensor_tensor(
+                out=inverse[:], in0=clamped[:], in1=minus_half[:], op=ALU.pow
+            )
+            inverse_norm[u] = inverse
+
+        def normalise_and_transpose(u):
+            unit_length = per_unit.tile([P, PAIR, EMB], BF16)
+            bank = flipped_banks.tile([P, PAIR, HALVES, P], F32)
+            words = unit_length[:].bitcast(F32)
+            for a in range(PAIR):
+                nc.vector.tensor_scalar(
+                    out=unit_length[:, a, :],
+                    in0=raw[u][:, a, :],
+                    scalar1=inverse_norm[u][:, a : a + 1],
+                    scalar2=None,
+                    op0=ALU.mult,
+                )
+            for a in range(PAIR):
+                for h in range(HALVES):
+                    nc.tensor.transpose(
+                        bank[:, a, h, :], words[:, a, h : HALVES * P : HALVES], identity[:]
+                    )
+            flipped[u] = bank
+
+        def evacuate(u):
+            side_by_side = per_unit.tile([P, UNIT_COLS * 4], BF16, align_bytes=64)
+            nc.vector.tensor_copy(
+                out=side_by_side[:].bitcast(F32).rearrange(
+                    "p (a r h) -> p a r h", a=PAIR, h=HALVES
+                ),
+                in_=flipped[u][:].rearrange("p a h r -> p a r h"),
+            )
+            grouped[u] = side_by_side
+
+        def quantise(u):
+            cols = slice(UNIT_COLS * u, UNIT_COLS * u + UNIT_COLS)
+            nc.vector.quantize_mx(
+                out=codes[:, cols].bitcast(FP8X4), scales=scales[:, cols], in_=grouped[u][:]
+            )
+
+        def multiply(b):
+            bank = cos_banks.tile([P, ITEM_TILES, USERS], F32)
+            user_cols = slice(P * b, P * b + P)
+            for c in range(ITEM_TILES):
+                t = BATCHES + ITEM_TILES * b + c
+                item_cols = slice(P * t, P * t + P)
+                nc.tensor.matmul_mx(
+                    out=bank[:, c, :],
+                    lhsT=codes[:, item_cols].bitcast(FP8X4),
+                    lhsT_scale=scales[:, item_cols],
+                    rhs=codes[:, user_cols].bitcast(FP8X4),
+                    rhs_scale=scales[:, user_cols],
+                    start=True,
+                    stop=True,
+                )
+            cos[b] = bank
+
+        def squash_and_store(b):
+            result = per_batch.tile([P, ITEM_TILES * USERS], F32)
+            nc.scalar.activation(
+                out=result[:],
+                in_=cos[b][:].rearrange("p c n -> p (c n)"),
+                func=ACT.Sigmoid,
+                bias=bias[:, 0:1],
+                scale=gain[:, 0:1],
+            )
+            nc.sync.dma_start(
+                out=out[b].rearrange("(p c) n -> p (c n)", c=ITEM_TILES), in_=result[:]
+            )
+
+        def is_unit(u):
+            return 0 <= u < UNITS
+
+        for u in range(UNITS):
+            load(u)
+
+        for step in range(UNITS + QUANTISE_LAG):
+            if is_unit(step):
+                squares(step)
+            if is_unit(step - INVERT_LAG):
+                invert(step - INVERT_LAG)
+            done = step - QUANTISE_LAG
+            if is_unit(done):
+                evacuate(done)
+            if is_unit(step - NORMALISE_LAG):
+                normalise_and_transpose(step - NORMALISE_LAG)
+            if is_unit(done):
+                quantise(done)
+                b, half = divmod(done - USER_UNITS, ITEM_TILES // PAIR)
+                if done >= USER_UNITS and half == ITEM_TILES // PAIR - 1:
+                    multiply(b)
+
+        for b in range(BATCHES):
+            squash_and_store(b)

@@ -25,12 +25,17 @@ ROW_TILES = BATCHES + BATCHES * ITEM_TILES
 PAIR = 2
 UNITS = ROW_TILES // PAIR
 USER_UNITS = BATCHES // PAIR
+UNITS_PER_BATCH = ITEM_TILES // PAIR
 HALVES = 2
+BLOCK = 32
+HALF_BLOCK = BLOCK // HALVES
+BLOCKS = EMB // BLOCK
 UNIT_COLS = PAIR * P
 
-INVERT_LAG = 1
-NORMALISE_LAG = 2
+NORMALISE_LAG = 1
+EVACUATE_LAG = 2
 QUANTISE_LAG = 3
+GAIN_STEP = 3
 
 
 def tile_similarityoutputlayer_s_kernel(tc, user_emb, item_emb, proj_w, proj_b, out):
@@ -39,56 +44,64 @@ def tile_similarityoutputlayer_s_kernel(tc, user_emb, item_emb, proj_w, proj_b, 
     def unit_rows(u):
         if u < USER_UNITS:
             return user_emb[PAIR * u : PAIR * u + PAIR].rearrange("b n k -> n b k")
-        b, half = divmod(u - USER_UNITS, ITEM_TILES // PAIR)
+        b, half = divmod(u - USER_UNITS, UNITS_PER_BATCH)
         by_partition = item_emb[b].rearrange("(p c) k -> p c k", c=ITEM_TILES)
         return by_partition[:, PAIR * half : PAIR * half + PAIR, :]
 
     with ExitStack() as ctx:
         const = ctx.enter_context(tc.tile_pool(name="const", bufs=1))
         per_unit = ctx.enter_context(tc.tile_pool(name="per_unit", bufs=UNITS))
-        per_batch = ctx.enter_context(tc.tile_pool(name="per_batch", bufs=BATCHES))
+        per_store = ctx.enter_context(tc.tile_pool(name="per_store", bufs=BATCHES + 1))
         flipped_banks = ctx.enter_context(tc.psum_pool(name="flipped_banks", bufs=4))
-        cos_banks = ctx.enter_context(tc.psum_pool(name="cos_banks", bufs=BATCHES))
+        cos_banks = ctx.enter_context(tc.psum_pool(name="cos_banks", bufs=4))
         ctx.enter_context(tc.manual_schedule())
+
+        raw, sum_squares, inverse_norm, flipped, grouped, cos = {}, {}, {}, {}, {}, {}
+
+        def load(u):
+            rows = per_unit.tile([P, PAIR, EMB], BF16)
+            if u == 0:
+                for a in range(PAIR):
+                    nc.sync.dma_start(out=rows[:, a, :], in_=unit_rows(u)[:, a, :])
+            else:
+                nc.sync.dma_start(out=rows[:], in_=unit_rows(u))
+            raw[u] = rows
+
+        for u in range(UNITS):
+            load(u)
 
         minus_half = const.tile([P, PAIR], F32)
         nc.gpsimd.memset(minus_half[:], -0.5)
-        identity = const.tile([P, P], F32)
-        make_identity(nc, identity[:])
         gain_bf16 = const.tile([P, 1], BF16)
-        nc.gpsimd.dma_start(
+        nc.sync.dma_start(
             out=gain_bf16[:], in_=proj_w.rearrange("a b -> (a b)").partition_broadcast(P)
         )
-        bias_bf16 = const.tile([P, 1], BF16)
-        nc.gpsimd.dma_start(out=bias_bf16[:], in_=proj_b.partition_broadcast(P))
+        bias = const.tile([P, 1], BF16)
+        nc.sync.dma_start(out=bias[:], in_=proj_b.partition_broadcast(P))
+        identity = const.tile([P, P], F32)
+        make_identity(nc, identity[:])
         table_warmer = const.tile([P, 1], F32)
         nc.scalar.activation(out=table_warmer[:], in_=minus_half[:, 0:1], func=ACT.Sigmoid)
         gain = const.tile([P, 1], F32)
-        nc.vector.tensor_copy(out=gain[:], in_=gain_bf16[:])
-        bias = const.tile([P, 1], F32)
-        nc.vector.tensor_copy(out=bias[:], in_=bias_bf16[:])
 
         codes = const.tile([P, ROW_TILES * P], U32, align_bytes=64)
         scales = const.tile([P, ROW_TILES * P], U8, align_bytes=64)
 
-        raw, inverse_norm, flipped, grouped = {}, {}, {}, {}
-        sum_squares, cos = {}, {}
-
-        def load(u):
-            rows = per_unit.tile([P, PAIR, EMB], BF16)
-            nc.sync.dma_start(out=rows[:], in_=unit_rows(u))
-            raw[u] = rows
-
         def squares(u):
             unread = per_unit.tile([P, PAIR, EMB], BF16)
             total = per_unit.tile([P, PAIR], F32)
-            for a in range(PAIR):
-                nc.scalar.activation(
-                    out=unread[:, a, :],
-                    in_=raw[u][:, a, :],
-                    func=ACT.Square,
-                    accum_out=total[:, a : a + 1],
-                )
+            nc.scalar.activation(
+                out=unread[:, 0, :], in_=raw[u][:, 0, :], func=ACT.Square, accum_out=total[:, 0:1]
+            )
+            nc.vector.scalar_tensor_tensor(
+                out=unread[:, 1, :],
+                in0=raw[u][:, 1, :],
+                scalar=1.0,
+                in1=raw[u][:, 1, :],
+                op0=ALU.mult,
+                op1=ALU.mult,
+                accum_out=total[:, 1:2],
+            )
             sum_squares[u] = total
 
         def invert(u):
@@ -106,8 +119,10 @@ def tile_similarityoutputlayer_s_kernel(tc, user_emb, item_emb, proj_w, proj_b, 
             words = unit_length[:].bitcast(F32)
             for a in range(PAIR):
                 nc.vector.tensor_scalar(
-                    out=unit_length[:, a, :],
-                    in0=raw[u][:, a, :],
+                    out=unit_length[:, a, :].rearrange(
+                        "p (h q w) -> p h q w", h=HALVES, w=HALF_BLOCK
+                    ),
+                    in0=raw[u][:, a, :].rearrange("p (q h w) -> p h q w", h=HALVES, w=HALF_BLOCK),
                     scalar1=inverse_norm[u][:, a : a + 1],
                     scalar2=None,
                     op0=ALU.mult,
@@ -115,13 +130,13 @@ def tile_similarityoutputlayer_s_kernel(tc, user_emb, item_emb, proj_w, proj_b, 
             for a in range(PAIR):
                 for h in range(HALVES):
                     nc.tensor.transpose(
-                        bank[:, a, h, :], words[:, a, h : HALVES * P : HALVES], identity[:]
+                        bank[:, a, h, :], words[:, a, P * h : P * h + P], identity[:]
                     )
             flipped[u] = bank
 
         def evacuate(u):
             side_by_side = per_unit.tile([P, UNIT_COLS * 4], BF16, align_bytes=64)
-            nc.vector.tensor_copy(
+            nc.scalar.copy(
                 out=side_by_side[:].bitcast(F32).rearrange(
                     "p (a r h) -> p a r h", a=PAIR, h=HALVES
                 ),
@@ -135,10 +150,10 @@ def tile_similarityoutputlayer_s_kernel(tc, user_emb, item_emb, proj_w, proj_b, 
                 out=codes[:, cols].bitcast(FP8X4), scales=scales[:, cols], in_=grouped[u][:]
             )
 
-        def multiply(b):
+        def multiply(b, tiles):
             bank = cos_banks.tile([P, ITEM_TILES, USERS], F32)
             user_cols = slice(P * b, P * b + P)
-            for c in range(ITEM_TILES):
+            for c in tiles:
                 t = BATCHES + ITEM_TILES * b + c
                 item_cols = slice(P * t, P * t + P)
                 nc.tensor.matmul_mx(
@@ -150,42 +165,52 @@ def tile_similarityoutputlayer_s_kernel(tc, user_emb, item_emb, proj_w, proj_b, 
                     start=True,
                     stop=True,
                 )
-            cos[b] = bank
+            cos[b, tiles.start] = bank
 
-        def squash_and_store(b):
-            result = per_batch.tile([P, ITEM_TILES * USERS], F32)
+        def squash_and_store(b, tiles):
+            result = per_store.tile([P, ITEM_TILES, USERS], F32)
+            span = slice(tiles.start, tiles.stop)
             nc.scalar.activation(
-                out=result[:],
-                in_=cos[b][:].rearrange("p c n -> p (c n)"),
+                out=result[:, span, :].rearrange("p c n -> p (c n)"),
+                in_=cos[b, tiles.start][:, span, :].rearrange("p c n -> p (c n)"),
                 func=ACT.Sigmoid,
                 bias=bias[:, 0:1],
                 scale=gain[:, 0:1],
             )
             nc.sync.dma_start(
-                out=out[b].rearrange("(p c) n -> p (c n)", c=ITEM_TILES), in_=result[:]
+                out=out[b].rearrange("(p c) n -> p c n", c=ITEM_TILES)[:, span, :],
+                in_=result[:, span, :],
             )
 
         def is_unit(u):
             return 0 <= u < UNITS
 
-        for u in range(UNITS):
-            load(u)
+        def squares_of(step):
+            return range(min(2 * step, UNITS), min(2 * step + 2, UNITS))
 
+        pending = []
         for step in range(UNITS + QUANTISE_LAG):
-            if is_unit(step):
-                squares(step)
-            if is_unit(step - INVERT_LAG):
-                invert(step - INVERT_LAG)
-            done = step - QUANTISE_LAG
-            if is_unit(done):
-                evacuate(done)
             if is_unit(step - NORMALISE_LAG):
                 normalise_and_transpose(step - NORMALISE_LAG)
+            done = step - QUANTISE_LAG
+            if is_unit(step - EVACUATE_LAG):
+                evacuate(step - EVACUATE_LAG)
+            for b, tiles in pending:
+                squash_and_store(b, tiles)
+            pending = []
+            for u in squares_of(step):
+                squares(u)
+                invert(u)
+            if step == GAIN_STEP:
+                nc.gpsimd.tensor_copy(out=gain[:], in_=gain_bf16[:])
             if is_unit(done):
                 quantise(done)
-                b, half = divmod(done - USER_UNITS, ITEM_TILES // PAIR)
-                if done >= USER_UNITS and half == ITEM_TILES // PAIR - 1:
-                    multiply(b)
-
-        for b in range(BATCHES):
-            squash_and_store(b)
+                b, half = divmod(done - USER_UNITS, UNITS_PER_BATCH)
+                if b == BATCHES - 1:
+                    pending.append((b, range(PAIR * half, PAIR * half + PAIR)))
+                elif b >= 0 and half == UNITS_PER_BATCH - 1:
+                    pending.append((b, range(ITEM_TILES)))
+                for mb, mtiles in pending:
+                    multiply(mb, mtiles)
+        for b, tiles in pending:
+            squash_and_store(b, tiles)

@@ -32,10 +32,18 @@ HALF_BLOCK = BLOCK // HALVES
 BLOCKS = EMB // BLOCK
 UNIT_COLS = PAIR * P
 
+GROUP = 2
+GROUPS = UNITS // GROUP
+GROUP_TILES = GROUP * PAIR
+
 NORMALISE_LAG = 1
 EVACUATE_LAG = 2
 QUANTISE_LAG = 3
-GAIN_STEP = 3
+SIGMOID_STEP = 7
+
+
+def vector_evacuates(u):
+    return u >= UNITS // 2 and u % 2 == 1
 
 
 def tile_similarityoutputlayer_s_kernel(tc, user_emb, item_emb, proj_w, proj_b, out):
@@ -51,6 +59,7 @@ def tile_similarityoutputlayer_s_kernel(tc, user_emb, item_emb, proj_w, proj_b, 
     with ExitStack() as ctx:
         const = ctx.enter_context(tc.tile_pool(name="const", bufs=1))
         per_unit = ctx.enter_context(tc.tile_pool(name="per_unit", bufs=UNITS))
+        per_group = ctx.enter_context(tc.tile_pool(name="per_group", bufs=GROUPS))
         per_store = ctx.enter_context(tc.tile_pool(name="per_store", bufs=BATCHES + 1))
         flipped_banks = ctx.enter_context(tc.psum_pool(name="flipped_banks", bufs=4))
         cos_banks = ctx.enter_context(tc.psum_pool(name="cos_banks", bufs=4))
@@ -70,8 +79,8 @@ def tile_similarityoutputlayer_s_kernel(tc, user_emb, item_emb, proj_w, proj_b, 
         for u in range(UNITS):
             load(u)
 
-        minus_half = const.tile([P, PAIR], F32)
-        nc.gpsimd.memset(minus_half[:], -0.5)
+        ones = const.tile([P, 1], F32)
+        nc.gpsimd.memset(ones[:], 1.0)
         gain_bf16 = const.tile([P, 1], BF16)
         nc.sync.dma_start(
             out=gain_bf16[:], in_=proj_w.rearrange("a b -> (a b)").partition_broadcast(P)
@@ -81,39 +90,45 @@ def tile_similarityoutputlayer_s_kernel(tc, user_emb, item_emb, proj_w, proj_b, 
         identity = const.tile([P, P], F32)
         make_identity(nc, identity[:])
         table_warmer = const.tile([P, 1], F32)
-        nc.scalar.activation(out=table_warmer[:], in_=minus_half[:, 0:1], func=ACT.Sigmoid)
+        nc.scalar.activation(out=table_warmer[:], in_=ones[:], func=ACT.Abs_reciprocal_sqrt)
         gain = const.tile([P, 1], F32)
+
+        nc.gpsimd.tensor_copy(out=gain[:], in_=gain_bf16[:])
 
         codes = const.tile([P, ROW_TILES * P], U32, align_bytes=64)
         scales = const.tile([P, ROW_TILES * P], U8, align_bytes=64)
 
-        def squares(u):
-            unread = per_unit.tile([P, PAIR, EMB], BF16)
-            total = per_unit.tile([P, PAIR], F32)
-            nc.scalar.activation(
-                out=unread[:, 0, :], in_=raw[u][:, 0, :], func=ACT.Square, accum_out=total[:, 0:1]
-            )
-            nc.vector.scalar_tensor_tensor(
-                out=unread[:, 1, :],
-                in0=raw[u][:, 1, :],
-                scalar=1.0,
-                in1=raw[u][:, 1, :],
-                op0=ALU.mult,
-                op1=ALU.mult,
-                accum_out=total[:, 1:2],
-            )
-            sum_squares[u] = total
+        def squares(g):
+            total = per_group.tile([P, GROUP_TILES], F32)
+            for i in range(GROUP):
+                u = GROUP * g + i
+                unread = per_unit.tile([P, PAIR, EMB], BF16)
+                nc.scalar.activation(
+                    out=unread[:, 0, :],
+                    in_=raw[u][:, 0, :],
+                    func=ACT.Square,
+                    accum_out=total[:, PAIR * i : PAIR * i + 1],
+                )
+                nc.vector.scalar_tensor_tensor(
+                    out=unread[:, 1, :],
+                    in0=raw[u][:, 1, :],
+                    scalar=1.0,
+                    in1=raw[u][:, 1, :],
+                    op0=ALU.mult,
+                    op1=ALU.mult,
+                    accum_out=total[:, PAIR * i + 1 : PAIR * i + 2],
+                )
+            sum_squares[g] = total
 
-        def invert(u):
-            clamped = per_unit.tile([P, PAIR], F32)
-            nc.gpsimd.tensor_scalar_max(out=clamped[:], in0=sum_squares[u][:], scalar1=EPS * EPS)
-            inverse = per_unit.tile([P, PAIR], F32)
-            nc.gpsimd.tensor_tensor(
-                out=inverse[:], in0=clamped[:], in1=minus_half[:], op=ALU.pow
-            )
-            inverse_norm[u] = inverse
+        def invert(g):
+            clamped = per_group.tile([P, GROUP_TILES], F32)
+            nc.vector.tensor_scalar_max(out=clamped[:], in0=sum_squares[g][:], scalar1=EPS * EPS)
+            inverse = per_group.tile([P, GROUP_TILES], F32)
+            nc.scalar.activation(out=inverse[:], in_=clamped[:], func=ACT.Abs_reciprocal_sqrt)
+            inverse_norm[g] = inverse
 
         def normalise_and_transpose(u):
+            g, i = divmod(u, GROUP)
             unit_length = per_unit.tile([P, PAIR, EMB], BF16)
             bank = flipped_banks.tile([P, PAIR, HALVES, P], F32)
             words = unit_length[:].bitcast(F32)
@@ -123,7 +138,7 @@ def tile_similarityoutputlayer_s_kernel(tc, user_emb, item_emb, proj_w, proj_b, 
                         "p (h q w) -> p h q w", h=HALVES, w=HALF_BLOCK
                     ),
                     in0=raw[u][:, a, :].rearrange("p (q h w) -> p h q w", h=HALVES, w=HALF_BLOCK),
-                    scalar1=inverse_norm[u][:, a : a + 1],
+                    scalar1=inverse_norm[g][:, PAIR * i + a : PAIR * i + a + 1],
                     scalar2=None,
                     op0=ALU.mult,
                 )
@@ -136,7 +151,8 @@ def tile_similarityoutputlayer_s_kernel(tc, user_emb, item_emb, proj_w, proj_b, 
 
         def evacuate(u):
             side_by_side = per_unit.tile([P, UNIT_COLS * 4], BF16, align_bytes=64)
-            nc.scalar.copy(
+            copy = nc.vector.tensor_copy if vector_evacuates(u) else nc.scalar.copy
+            copy(
                 out=side_by_side[:].bitcast(F32).rearrange(
                     "p (a r h) -> p a r h", a=PAIR, h=HALVES
                 ),
@@ -185,24 +201,22 @@ def tile_similarityoutputlayer_s_kernel(tc, user_emb, item_emb, proj_w, proj_b, 
         def is_unit(u):
             return 0 <= u < UNITS
 
-        def squares_of(step):
-            return range(min(2 * step, UNITS), min(2 * step + 2, UNITS))
-
         pending = []
         for step in range(UNITS + QUANTISE_LAG):
+            if step == SIGMOID_STEP:
+                nc.scalar.activation(out=table_warmer[:], in_=ones[:], func=ACT.Sigmoid)
+            if step < GROUPS:
+                squares(step)
             if is_unit(step - NORMALISE_LAG):
                 normalise_and_transpose(step - NORMALISE_LAG)
-            done = step - QUANTISE_LAG
             if is_unit(step - EVACUATE_LAG):
                 evacuate(step - EVACUATE_LAG)
             for b, tiles in pending:
                 squash_and_store(b, tiles)
             pending = []
-            for u in squares_of(step):
-                squares(u)
-                invert(u)
-            if step == GAIN_STEP:
-                nc.gpsimd.tensor_copy(out=gain[:], in_=gain_bf16[:])
+            if step < GROUPS:
+                invert(step)
+            done = step - QUANTISE_LAG
             if is_unit(done):
                 quantise(done)
                 b, half = divmod(done - USER_UNITS, UNITS_PER_BATCH)

@@ -36,14 +36,15 @@ GROUP = 2
 GROUPS = UNITS // GROUP
 GROUP_TILES = GROUP * PAIR
 
-NORMALISE_LAG = 1
-EVACUATE_LAG = 2
-QUANTISE_LAG = 3
-SIGMOID_STEP = 7
+INVERT_LAG = 1
+NORMALISE_LAG = 2
+EVACUATE_LAG = 3
+QUANTISE_LAG = 5
+SIGMOID_STEP = 9
 
 
 def vector_evacuates(u):
-    return u >= UNITS // 2 and u % 2 == 1
+    return u > UNITS // 2 and u % 2 == 0
 
 
 def tile_similarityoutputlayer_s_kernel(tc, user_emb, item_emb, proj_w, proj_b, out):
@@ -98,34 +99,38 @@ def tile_similarityoutputlayer_s_kernel(tc, user_emb, item_emb, proj_w, proj_b, 
         codes = const.tile([P, ROW_TILES * P], U32, align_bytes=64)
         scales = const.tile([P, ROW_TILES * P], U8, align_bytes=64)
 
-        def squares(g):
-            total = per_group.tile([P, GROUP_TILES], F32)
-            for i in range(GROUP):
-                u = GROUP * g + i
-                unread = per_unit.tile([P, PAIR, EMB], BF16)
-                nc.scalar.activation(
-                    out=unread[:, 0, :],
-                    in_=raw[u][:, 0, :],
-                    func=ACT.Square,
-                    accum_out=total[:, PAIR * i : PAIR * i + 1],
-                )
-                nc.vector.scalar_tensor_tensor(
-                    out=unread[:, 1, :],
-                    in0=raw[u][:, 1, :],
-                    scalar=1.0,
-                    in1=raw[u][:, 1, :],
-                    op0=ALU.mult,
-                    op1=ALU.mult,
-                    accum_out=total[:, PAIR * i + 1 : PAIR * i + 2],
-                )
-            sum_squares[g] = total
+        def squares(u):
+            g, i = divmod(u, GROUP)
+            if i == 0:
+                sum_squares[g] = per_group.tile([P, GROUP_TILES], F32, name="total")
+            total = sum_squares[g][:, PAIR * i : PAIR * i + PAIR]
+            unread = per_unit.tile([P, PAIR, EMB], BF16)
+            nc.scalar.activation(
+                out=unread[:, 0, :], in_=raw[u][:, 0, :], func=ACT.Square, accum_out=total[:, 0:1]
+            )
+            nc.vector.scalar_tensor_tensor(
+                out=unread[:, 1, :],
+                in0=raw[u][:, 1, :],
+                scalar=1.0,
+                in1=raw[u][:, 1, :],
+                op0=ALU.mult,
+                op1=ALU.mult,
+                accum_out=total[:, 1:2],
+            )
 
         def invert(g):
-            clamped = per_group.tile([P, GROUP_TILES], F32)
-            nc.vector.tensor_scalar_max(out=clamped[:], in0=sum_squares[g][:], scalar1=EPS * EPS)
             inverse = per_group.tile([P, GROUP_TILES], F32)
-            nc.scalar.activation(out=inverse[:], in_=clamped[:], func=ACT.Abs_reciprocal_sqrt)
+            nc.scalar.activation(
+                out=inverse[:], in_=sum_squares[g][:], func=ACT.Abs_reciprocal_sqrt
+            )
             inverse_norm[g] = inverse
+
+        def clamp(g):
+            clamped = per_group.tile([P, GROUP_TILES], F32)
+            nc.vector.tensor_scalar_min(
+                out=clamped[:], in0=inverse_norm[g][:], scalar1=1.0 / EPS
+            )
+            inverse_norm[g] = clamped
 
         def normalise_and_transpose(u):
             g, i = divmod(u, GROUP)
@@ -205,8 +210,12 @@ def tile_similarityoutputlayer_s_kernel(tc, user_emb, item_emb, proj_w, proj_b, 
         for step in range(UNITS + QUANTISE_LAG):
             if step == SIGMOID_STEP:
                 nc.scalar.activation(out=table_warmer[:], in_=ones[:], func=ACT.Sigmoid)
-            if step < GROUPS:
-                squares(step)
+            first, second = GROUP * step, GROUP * step + 1
+            inverted = step - INVERT_LAG
+            if is_unit(first):
+                squares(first)
+            if 0 <= inverted < GROUPS:
+                invert(inverted)
             if is_unit(step - NORMALISE_LAG):
                 normalise_and_transpose(step - NORMALISE_LAG)
             if is_unit(step - EVACUATE_LAG):
@@ -214,8 +223,10 @@ def tile_similarityoutputlayer_s_kernel(tc, user_emb, item_emb, proj_w, proj_b, 
             for b, tiles in pending:
                 squash_and_store(b, tiles)
             pending = []
-            if step < GROUPS:
-                invert(step)
+            if is_unit(second):
+                squares(second)
+            if 0 <= inverted < GROUPS:
+                clamp(inverted)
             done = step - QUANTISE_LAG
             if is_unit(done):
                 quantise(done)

@@ -38,8 +38,8 @@ GROUP_TILES = GROUP * PAIR
 
 INVERT_LAG = 1
 NORMALISE_LAG = 2
-EVACUATE_LAG = 3
-QUANTISE_LAG = 5
+EVACUATE_LAG = 4
+QUANTISE_LAG = 7
 SIGMOID_STEP = 9
 
 

@@ -36,15 +36,13 @@ GROUP = 2
 GROUPS = UNITS // GROUP
 GROUP_TILES = GROUP * PAIR
 
-INVERT_LAG = 1
 NORMALISE_LAG = 2
 EVACUATE_LAG = 4
-QUANTISE_LAG = 7
-SIGMOID_STEP = 9
+QUANTISE_LAG = 6
 
 
 def vector_evacuates(u):
-    return u > UNITS // 2 and u % 2 == 0
+    return u > UNITS // 2 and u % 2 == 1
 
 
 def tile_similarityoutputlayer_s_kernel(tc, user_emb, item_emb, proj_w, proj_b, out):
@@ -80,8 +78,8 @@ def tile_similarityoutputlayer_s_kernel(tc, user_emb, item_emb, proj_w, proj_b, 
         for u in range(UNITS):
             load(u)
 
-        ones = const.tile([P, 1], F32)
-        nc.gpsimd.memset(ones[:], 1.0)
+        minus_half = const.tile([P, GROUP_TILES], F32)
+        nc.gpsimd.memset(minus_half[:], -0.5)
         gain_bf16 = const.tile([P, 1], BF16)
         nc.sync.dma_start(
             out=gain_bf16[:], in_=proj_w.rearrange("a b -> (a b)").partition_broadcast(P)
@@ -91,10 +89,8 @@ def tile_similarityoutputlayer_s_kernel(tc, user_emb, item_emb, proj_w, proj_b, 
         identity = const.tile([P, P], F32)
         make_identity(nc, identity[:])
         table_warmer = const.tile([P, 1], F32)
-        nc.scalar.activation(out=table_warmer[:], in_=ones[:], func=ACT.Abs_reciprocal_sqrt)
+        nc.scalar.activation(out=table_warmer[:], in_=minus_half[:, 0:1], func=ACT.Sigmoid)
         gain = const.tile([P, 1], F32)
-
-        nc.gpsimd.tensor_copy(out=gain[:], in_=gain_bf16[:])
 
         codes = const.tile([P, ROW_TILES * P], U32, align_bytes=64)
         scales = const.tile([P, ROW_TILES * P], U8, align_bytes=64)
@@ -120,8 +116,8 @@ def tile_similarityoutputlayer_s_kernel(tc, user_emb, item_emb, proj_w, proj_b, 
 
         def invert(g):
             inverse = per_group.tile([P, GROUP_TILES], F32)
-            nc.scalar.activation(
-                out=inverse[:], in_=sum_squares[g][:], func=ACT.Abs_reciprocal_sqrt
+            nc.gpsimd.tensor_tensor(
+                out=inverse[:], in0=sum_squares[g][:], in1=minus_half[:], op=ALU.pow
             )
             inverse_norm[g] = inverse
 
@@ -206,36 +202,35 @@ def tile_similarityoutputlayer_s_kernel(tc, user_emb, item_emb, proj_w, proj_b, 
         def is_unit(u):
             return 0 <= u < UNITS
 
-        pending = []
+        finished = []
         for step in range(UNITS + QUANTISE_LAG):
-            if step == SIGMOID_STEP:
-                nc.scalar.activation(out=table_warmer[:], in_=ones[:], func=ACT.Sigmoid)
             first, second = GROUP * step, GROUP * step + 1
-            inverted = step - INVERT_LAG
             if is_unit(first):
                 squares(first)
-            if 0 <= inverted < GROUPS:
-                invert(inverted)
-            if is_unit(step - NORMALISE_LAG):
-                normalise_and_transpose(step - NORMALISE_LAG)
-            if is_unit(step - EVACUATE_LAG):
-                evacuate(step - EVACUATE_LAG)
-            for b, tiles in pending:
-                squash_and_store(b, tiles)
-            pending = []
+            g, i = divmod(step - NORMALISE_LAG, GROUP)
+            if 0 <= g < GROUPS and i == 0:
+                clamp(g)
             if is_unit(second):
                 squares(second)
-            if 0 <= inverted < GROUPS:
-                clamp(inverted)
+                invert(step)
+            if step == GROUPS:
+                nc.gpsimd.tensor_copy(out=gain[:], in_=gain_bf16[:])
+            ready, finished = finished, []
             done = step - QUANTISE_LAG
             if is_unit(done):
                 quantise(done)
                 b, half = divmod(done - USER_UNITS, UNITS_PER_BATCH)
                 if b == BATCHES - 1:
-                    pending.append((b, range(PAIR * half, PAIR * half + PAIR)))
+                    finished.append((b, range(PAIR * half, PAIR * half + PAIR)))
                 elif b >= 0 and half == UNITS_PER_BATCH - 1:
-                    pending.append((b, range(ITEM_TILES)))
-                for mb, mtiles in pending:
-                    multiply(mb, mtiles)
-        for b, tiles in pending:
+                    finished.append((b, range(ITEM_TILES)))
+            if is_unit(step - NORMALISE_LAG):
+                normalise_and_transpose(step - NORMALISE_LAG)
+            for b, tiles in finished:
+                multiply(b, tiles)
+            if is_unit(step - EVACUATE_LAG):
+                evacuate(step - EVACUATE_LAG)
+            for b, tiles in ready:
+                squash_and_store(b, tiles)
+        for b, tiles in finished:
             squash_and_store(b, tiles)

@@ -37,7 +37,8 @@ GROUPS = UNITS // GROUP
 GROUP_TILES = GROUP * PAIR
 
 NORMALISE_LAG = 2
-EVACUATE_LAG = 4
+SCALAR_EVACUATE_LAG = 3
+VECTOR_EVACUATE_LAG = 4
 QUANTISE_LAG = 6
 
 
@@ -104,15 +105,23 @@ def tile_similarityoutputlayer_s_kernel(tc, user_emb, item_emb, proj_w, proj_b, 
             nc.scalar.activation(
                 out=unread[:, 0, :], in_=raw[u][:, 0, :], func=ACT.Square, accum_out=total[:, 0:1]
             )
-            nc.vector.scalar_tensor_tensor(
-                out=unread[:, 1, :],
-                in0=raw[u][:, 1, :],
-                scalar=1.0,
-                in1=raw[u][:, 1, :],
-                op0=ALU.mult,
-                op1=ALU.mult,
-                accum_out=total[:, 1:2],
-            )
+            if u == UNITS - 1:
+                nc.scalar.activation(
+                    out=unread[:, 1, :],
+                    in_=raw[u][:, 1, :],
+                    func=ACT.Square,
+                    accum_out=total[:, 1:2],
+                )
+            else:
+                nc.vector.scalar_tensor_tensor(
+                    out=unread[:, 1, :],
+                    in0=raw[u][:, 1, :],
+                    scalar=1.0,
+                    in1=raw[u][:, 1, :],
+                    op0=ALU.mult,
+                    op1=ALU.mult,
+                    accum_out=total[:, 1:2],
+                )
 
         def invert(g):
             inverse = per_group.tile([P, GROUP_TILES], F32)
@@ -228,8 +237,12 @@ def tile_similarityoutputlayer_s_kernel(tc, user_emb, item_emb, proj_w, proj_b, 
                 normalise_and_transpose(step - NORMALISE_LAG)
             for b, tiles in finished:
                 multiply(b, tiles)
-            if is_unit(step - EVACUATE_LAG):
-                evacuate(step - EVACUATE_LAG)
+            u = step - VECTOR_EVACUATE_LAG
+            if is_unit(u) and vector_evacuates(u):
+                evacuate(u)
+            u = step - SCALAR_EVACUATE_LAG
+            if is_unit(u) and not vector_evacuates(u):
+                evacuate(u)
             for b, tiles in ready:
                 squash_and_store(b, tiles)
         for b, tiles in finished:

@@ -33,6 +33,7 @@ BLOCKS = EMB // BLOCK
 UNIT_COLS = PAIR * P
 
 GROUP = 2
+SCALAR_SQUARES = UNITS - 2
 GROUPS = UNITS // GROUP
 GROUP_TILES = GROUP * PAIR
 
@@ -59,6 +60,7 @@ def tile_similarityoutputlayer_s_kernel(tc, user_emb, item_emb, proj_w, proj_b, 
     with ExitStack() as ctx:
         const = ctx.enter_context(tc.tile_pool(name="const", bufs=1))
         per_unit = ctx.enter_context(tc.tile_pool(name="per_unit", bufs=UNITS))
+        per_tile = ctx.enter_context(tc.tile_pool(name="per_tile", bufs=ROW_TILES))
         per_group = ctx.enter_context(tc.tile_pool(name="per_group", bufs=GROUPS))
         per_store = ctx.enter_context(tc.tile_pool(name="per_store", bufs=BATCHES + 1))
         flipped_banks = ctx.enter_context(tc.psum_pool(name="flipped_banks", bufs=4))
@@ -96,32 +98,31 @@ def tile_similarityoutputlayer_s_kernel(tc, user_emb, item_emb, proj_w, proj_b, 
         codes = const.tile([P, ROW_TILES * P], U32, align_bytes=64)
         scales = const.tile([P, ROW_TILES * P], U8, align_bytes=64)
 
-        def squares(u):
+        def square(u, a, engine):
             g, i = divmod(u, GROUP)
-            if i == 0:
+            if g not in sum_squares:
                 sum_squares[g] = per_group.tile([P, GROUP_TILES], F32, name="total")
-            total = sum_squares[g][:, PAIR * i : PAIR * i + PAIR]
-            unread = per_unit.tile([P, PAIR, EMB], BF16)
-            nc.scalar.activation(
-                out=unread[:, 0, :], in_=raw[u][:, 0, :], func=ACT.Square, accum_out=total[:, 0:1]
-            )
-            if u == UNITS - 1:
-                nc.scalar.activation(
-                    out=unread[:, 1, :],
-                    in_=raw[u][:, 1, :],
-                    func=ACT.Square,
-                    accum_out=total[:, 1:2],
-                )
+            column = PAIR * i + a
+            total = sum_squares[g][:, column : column + 1]
+            unread = per_tile.tile([P, EMB], BF16)
+            rows = raw[u][:, a, :]
+            if engine == "scalar":
+                nc.scalar.activation(out=unread[:], in_=rows, func=ACT.Square, accum_out=total)
             else:
                 nc.vector.scalar_tensor_tensor(
-                    out=unread[:, 1, :],
-                    in0=raw[u][:, 1, :],
+                    out=unread[:],
+                    in0=rows,
                     scalar=1.0,
-                    in1=raw[u][:, 1, :],
+                    in1=rows,
                     op0=ALU.mult,
                     op1=ALU.mult,
-                    accum_out=total[:, 1:2],
+                    accum_out=total,
                 )
+
+        def squares(u):
+            square(u, 0, "scalar")
+            if u != SCALAR_SQUARES:
+                square(u, 1, "vector")
 
         def invert(g):
             inverse = per_group.tile([P, GROUP_TILES], F32)
@@ -221,9 +222,6 @@ def tile_similarityoutputlayer_s_kernel(tc, user_emb, item_emb, proj_w, proj_b, 
                 clamp(g)
             if is_unit(second):
                 squares(second)
-                invert(step)
-            if step == GROUPS:
-                nc.gpsimd.tensor_copy(out=gain[:], in_=gain_bf16[:])
             ready, finished = finished, []
             done = step - QUANTISE_LAG
             if is_unit(done):
@@ -243,6 +241,12 @@ def tile_similarityoutputlayer_s_kernel(tc, user_emb, item_emb, proj_w, proj_b, 
             u = step - SCALAR_EVACUATE_LAG
             if is_unit(u) and not vector_evacuates(u):
                 evacuate(u)
+            if SCALAR_SQUARES in (first, second):
+                square(SCALAR_SQUARES, 1, "scalar")
+            if is_unit(second):
+                invert(step)
+            if step == GROUPS:
+                nc.gpsimd.tensor_copy(out=gain[:], in_=gain_bf16[:])
             for b, tiles in ready:
                 squash_and_store(b, tiles)
         for b, tiles in finished:

from contextlib import ExitStack

import concourse.mybir as mybir
from concourse.masks import make_identity

F32 = mybir.dt.float32
BF16 = mybir.dt.bfloat16
U32 = mybir.dt.uint32
U8 = mybir.dt.uint8
FP8X4 = mybir.dt.float8_e4m3fn_x4
ACT = mybir.ActivationFunctionType
ALU = mybir.AluOpType

P = 128
BATCHES = 4
USERS = 128
ITEMS = 512
EMB = 512
EPS = 1e-07

FLOPS = 2 * BATCHES * ITEMS * USERS * EMB

ITEM_TILES = ITEMS // P
ROW_TILES = BATCHES + BATCHES * ITEM_TILES
PAIR = 2
UNITS = ROW_TILES // PAIR
USER_UNITS = BATCHES // PAIR
UNITS_PER_BATCH = ITEM_TILES // PAIR
HALVES = 2
BLOCK = 32
HALF_BLOCK = BLOCK // HALVES
BLOCKS = EMB // BLOCK
UNIT_COLS = PAIR * P

GROUP = 2
SCALAR_SQUARES = UNITS - 2
GROUPS = UNITS // GROUP
GROUP_TILES = GROUP * PAIR

NORMALISE_LAG = 2
SCALAR_EVACUATE_LAG = 3
VECTOR_EVACUATE_LAG = 4
QUANTISE_LAG = 6


def vector_evacuates(u):
    return u > UNITS // 2 and u % 2 == 1


def tile_similarityoutputlayer_s_kernel(tc, user_emb, item_emb, proj_w, proj_b, out):
    nc = tc.nc

    def unit_rows(u):
        if u < USER_UNITS:
            return user_emb[PAIR * u : PAIR * u + PAIR].rearrange("b n k -> n b k")
        b, half = divmod(u - USER_UNITS, UNITS_PER_BATCH)
        by_partition = item_emb[b].rearrange("(p c) k -> p c k", c=ITEM_TILES)
        return by_partition[:, PAIR * half : PAIR * half + PAIR, :]

    with ExitStack() as ctx:
        const = ctx.enter_context(tc.tile_pool(name="const", bufs=1))
        per_unit = ctx.enter_context(tc.tile_pool(name="per_unit", bufs=UNITS))
        per_tile = ctx.enter_context(tc.tile_pool(name="per_tile", bufs=ROW_TILES))
        per_group = ctx.enter_context(tc.tile_pool(name="per_group", bufs=GROUPS))
        per_store = ctx.enter_context(tc.tile_pool(name="per_store", bufs=BATCHES + 1))
        flipped_banks = ctx.enter_context(tc.psum_pool(name="flipped_banks", bufs=4))
        cos_banks = ctx.enter_context(tc.psum_pool(name="cos_banks", bufs=4))
        ctx.enter_context(tc.manual_schedule())

        raw, sum_squares, inverse_norm, flipped, grouped, cos = {}, {}, {}, {}, {}, {}

        def load(u):
            rows = per_unit.tile([P, PAIR, EMB], BF16)
            if u == 0:
                for a in range(PAIR):
                    nc.sync.dma_start(out=rows[:, a, :], in_=unit_rows(u)[:, a, :])
            else:
                nc.sync.dma_start(out=rows[:], in_=unit_rows(u))
            raw[u] = rows

        for u in range(UNITS):
            load(u)

        minus_half = const.tile([P, GROUP_TILES], F32)
        nc.gpsimd.memset(minus_half[:], -0.5)
        gain_bf16 = const.tile([P, 1], BF16)
        nc.sync.dma_start(
            out=gain_bf16[:], in_=proj_w.rearrange("a b -> (a b)").partition_broadcast(P)
        )
        bias = const.tile([P, 1], BF16)
        nc.sync.dma_start(out=bias[:], in_=proj_b.partition_broadcast(P))
        identity = const.tile([P, P], F32)
        make_identity(nc, identity[:])
        table_warmer = const.tile([P, 1], F32)
        nc.scalar.activation(out=table_warmer[:], in_=minus_half[:, 0:1], func=ACT.Sigmoid)
        gain = const.tile([P, 1], F32)

        codes = const.tile([P, ROW_TILES * P], U32, align_bytes=64)
        scales = const.tile([P, ROW_TILES * P], U8, align_bytes=64)

        def square(u, a, engine):
            g, i = divmod(u, GROUP)
            if g not in sum_squares:
                sum_squares[g] = per_group.tile([P, GROUP_TILES], F32, name="total")
            column = PAIR * i + a
            total = sum_squares[g][:, column : column + 1]
            unread = per_tile.tile([P, EMB], BF16)
            rows = raw[u][:, a, :]
            if engine == "scalar":
                nc.scalar.activation(out=unread[:], in_=rows, func=ACT.Square, accum_out=total)
            else:
                nc.vector.scalar_tensor_tensor(
                    out=unread[:],
                    in0=rows,
                    scalar=1.0,
                    in1=rows,
                    op0=ALU.mult,
                    op1=ALU.mult,
                    accum_out=total,
                )

        def squares(u):
            square(u, 0, "scalar")
            if u != SCALAR_SQUARES:
                square(u, 1, "vector")

        def invert(g):
            inverse = per_group.tile([P, GROUP_TILES], F32)
            nc.gpsimd.tensor_tensor(
                out=inverse[:], in0=sum_squares[g][:], in1=minus_half[:], op=ALU.pow
            )
            inverse_norm[g] = inverse

        def clamp(g):
            clamped = per_group.tile([P, GROUP_TILES], F32)
            nc.vector.tensor_scalar_min(
                out=clamped[:], in0=inverse_norm[g][:], scalar1=1.0 / EPS
            )
            inverse_norm[g] = clamped

        def normalise_and_transpose(u):
            g, i = divmod(u, GROUP)
            unit_length = per_unit.tile([P, PAIR, EMB], BF16)
            bank = flipped_banks.tile([P, PAIR, HALVES, P], F32)
            words = unit_length[:].bitcast(F32)
            for a in range(PAIR):
                nc.vector.tensor_scalar(
                    out=unit_length[:, a, :].rearrange(
                        "p (h q w) -> p h q w", h=HALVES, w=HALF_BLOCK
                    ),
                    in0=raw[u][:, a, :].rearrange("p (q h w) -> p h q w", h=HALVES, w=HALF_BLOCK),
                    scalar1=inverse_norm[g][:, PAIR * i + a : PAIR * i + a + 1],
                    scalar2=None,
                    op0=ALU.mult,
                )
            for a in range(PAIR):
                for h in range(HALVES):
                    nc.tensor.transpose(
                        bank[:, a, h, :], words[:, a, P * h : P * h + P], identity[:]
                    )
            flipped[u] = bank

        def evacuate(u):
            side_by_side = per_unit.tile([P, UNIT_COLS * 4], BF16, align_bytes=64)
            copy = nc.vector.tensor_copy if vector_evacuates(u) else nc.scalar.copy
            copy(
                out=side_by_side[:].bitcast(F32).rearrange(
                    "p (a r h) -> p a r h", a=PAIR, h=HALVES
                ),
                in_=flipped[u][:].rearrange("p a h r -> p a r h"),
            )
            grouped[u] = side_by_side

        def quantise(u):
            cols = slice(UNIT_COLS * u, UNIT_COLS * u + UNIT_COLS)
            nc.vector.quantize_mx(
                out=codes[:, cols].bitcast(FP8X4), scales=scales[:, cols], in_=grouped[u][:]
            )

        def multiply(b, tiles):
            bank = cos_banks.tile([P, ITEM_TILES, USERS], F32)
            user_cols = slice(P * b, P * b + P)
            for c in tiles:
                t = BATCHES + ITEM_TILES * b + c
                item_cols = slice(P * t, P * t + P)
                nc.tensor.matmul_mx(
                    out=bank[:, c, :],
                    lhsT=codes[:, item_cols].bitcast(FP8X4),
                    lhsT_scale=scales[:, item_cols],
                    rhs=codes[:, user_cols].bitcast(FP8X4),
                    rhs_scale=scales[:, user_cols],
                    start=True,
                    stop=True,
                )
            cos[b, tiles.start] = bank

        def squash_and_store(b, tiles):
            result = per_store.tile([P, ITEM_TILES, USERS], F32)
            span = slice(tiles.start, tiles.stop)
            nc.scalar.activation(
                out=result[:, span, :].rearrange("p c n -> p (c n)"),
                in_=cos[b, tiles.start][:, span, :].rearrange("p c n -> p (c n)"),
                func=ACT.Sigmoid,
                bias=bias[:, 0:1],
                scale=gain[:, 0:1],
            )
            nc.sync.dma_start(
                out=out[b].rearrange("(p c) n -> p c n", c=ITEM_TILES)[:, span, :],
                in_=result[:, span, :],
            )

        def is_unit(u):
            return 0 <= u < UNITS

        finished = []
        for step in range(UNITS + QUANTISE_LAG):
            first, second = GROUP * step, GROUP * step + 1
            if is_unit(first):
                squares(first)
            g, i = divmod(step - NORMALISE_LAG, GROUP)
            if 0 <= g < GROUPS and i == 0:
                clamp(g)
            if is_unit(second):
                squares(second)
            ready, finished = finished, []
            done = step - QUANTISE_LAG
            if is_unit(done):
                quantise(done)
                b, half = divmod(done - USER_UNITS, UNITS_PER_BATCH)
                if b == BATCHES - 1:
                    finished.append((b, range(PAIR * half, PAIR * half + PAIR)))
                elif b >= 0 and half == UNITS_PER_BATCH - 1:
                    finished.append((b, range(ITEM_TILES)))
            if is_unit(step - NORMALISE_LAG):
                normalise_and_transpose(step - NORMALISE_LAG)
            for b, tiles in finished:
                multiply(b, tiles)
            u = step - VECTOR_EVACUATE_LAG
            if is_unit(u) and vector_evacuates(u):
                evacuate(u)
            u = step - SCALAR_EVACUATE_LAG
            if is_unit(u) and not vector_evacuates(u):
                evacuate(u)
            if SCALAR_SQUARES in (first, second):
                square(SCALAR_SQUARES, 1, "scalar")
            if is_unit(second):
                invert(step)
            if step == GROUPS:
                nc.gpsimd.tensor_copy(out=gain[:], in_=gain_bf16[:])
            for b, tiles in ready:
                squash_and_store(b, tiles)
        for b, tiles in finished:
            squash_and_store(b, tiles)
